import numpy as np
import ml_dtypes


def mxq(x, axis, fmt="e4m3"):
    dtype, down = {"e4m3": (ml_dtypes.float8_e4m3fn, 7), "e5m2": (ml_dtypes.float8_e5m2, 14)}[fmt]
    v = np.moveaxis(np.asarray(x, np.float32).astype(ml_dtypes.bfloat16).astype(np.float64), axis, -1)
    blocks = v.reshape(v.shape[:-1] + (-1, 32))
    amax = np.abs(blocks).max(-1, keepdims=True)
    byte = np.maximum(np.where(amax > 0, np.frexp(amax)[1] - 1 + 127, 0) - down, 1)
    scale = np.exp2(byte - 127.0)
    codes = (blocks / scale).astype(np.float32).astype(dtype).astype(np.float64)
    return np.moveaxis((codes * scale).reshape(v.shape), -1, axis)


WIDE = False


def mx_kscale(k):
    if not WIDE:
        return np.ones(k)
    levels = np.array([10, -10, 5, -5, 0])
    a = np.random.permutation(np.resize(levels, k // 512 * 4)).reshape(k // 512, 4)
    idx = np.arange(k)
    return np.exp2(a[idx // 512, idx % 128 // 32])


BF16 = ml_dtypes.bfloat16


def bf(x):
    return np.asarray(x, np.float32).astype(BF16)


def f64(x):
    return np.asarray(x).astype(np.float64)


B, D, H = 8192, 512, 8
DH = D // H
LN_EPS = 1e-5


def layernorm(x, g, b):
    mu = x.mean(-1, keepdims=True)
    var = ((x - mu) ** 2).mean(-1, keepdims=True)
    return (x - mu) / np.sqrt(var + LN_EPS) * g + b


def setup_inputs():
    s, t = mx_kscale(D), mx_kscale(D)
    return {"kv_in": bf(np.random.standard_normal((B, D)) * s),
            "q_in": bf(np.random.standard_normal((B, D))),
            "attn_w": bf(np.random.uniform(0.25, 1.0, (B, H, 1))),
            "w_v": bf(np.random.standard_normal((D, D)) / np.sqrt(D) / s[None, :] * t[:, None]),
            "b_v": bf(np.random.standard_normal(D) * 0.3 * t),
            "out_w": bf(np.random.standard_normal((D, D)) / np.sqrt(D) / t[None, :]),
            "out_b": bf(np.random.standard_normal(D) * 0.3),
            "ln_g": bf(1.0 + 0.1 * np.random.standard_normal(D)),
            "ln_b": bf(0.1 * np.random.standard_normal(D))}


def reference(kv_in, q_in, attn_w, w_v, b_v, out_w, out_b, ln_g, ln_b):
    v = ((mxq(f64(kv_in), 1, "e4m3") @ mxq(f64(w_v), 1, "e4m3").T) + f64(b_v)).reshape(B, H, DH)
    attn = (f64(attn_w) * v).reshape(B, D)
    y = (mxq(attn, 1, "e4m3") @ mxq(f64(out_w), 1, "e4m3").T) + f64(out_b)
    return layernorm(y + f64(q_in), f64(ln_g), f64(ln_b))

@@ -1,0 +1,331 @@
+from contextlib import ExitStack
+
+import concourse.mybir as mybir
+from concourse.masks import make_identity
+
+F32 = mybir.dt.float32
+BF16 = mybir.dt.bfloat16
+U32 = mybir.dt.uint32
+U8 = mybir.dt.uint8
+FP8X4 = mybir.dt.float8_e4m3fn_x4
+ALU = mybir.AluOpType
+ACT = mybir.ActivationFunctionType
+
+P = 128
+B = 8192
+D = 512
+NT = B // P
+GT = 2
+NG = NT // GT
+GW = GT * D
+GC = GT * P
+BLK = 8
+LN_EPS = 1e-5
+FLOPS = 2 * 2 * B * D * D
+PINNED = True
+
+
+def tile_crossmodalattention_pa_t_kernel(
+    tc, kv_in, q_in, attn_w, w_v, b_v, out_w, out_b, ln_g, ln_b, out
+):
+    nc = tc.nc
+    with ExitStack() as ctx:
+        if PINNED:
+            ctx.enter_context(tc.manual_schedule())
+        const = ctx.enter_context(tc.tile_pool(name="const", bufs=1))
+        w2 = ctx.enter_context(tc.tile_pool(name="w2", bufs=2))
+        w3 = ctx.enter_context(tc.tile_pool(name="w3", bufs=3))
+        psum = ctx.enter_context(tc.psum_pool(name="psum", bufs=1))
+
+        kv_view = kv_in.rearrange("(p j) k -> p (j k)", j=NT)
+        q_view = q_in.rearrange("(p j) k -> p (j k)", j=NT)
+        out_view = out.rearrange("(p j) n -> p (j n)", j=NT)
+
+        chunks = [(0, 2), (2, 8)] + [(a, a + 8) for a in range(8, NT, 8)]
+        kv_tiles = {}
+        q_tiles = {}
+
+        def load_chunk(view, store, prefix, k):
+            j0, j1 = chunks[k]
+            t = const.tile([P, (j1 - j0) * D], BF16, name="%s%d" % (prefix, k))
+            nc.sync.dma_start(out=t[:], in_=view[:, j0 * D : j1 * D])
+            for j in range(j0, j1):
+                store[j] = (t, (j - j0) * D)
+
+        eps = const.tile([P, 1], F32, name="eps")
+        nc.vector.memset(eps[:], LN_EPS)
+        warm = const.tile([P, 1], F32, name="warm")
+        nc.scalar.activation(out=warm[:], in_=eps[:], func=ACT.Sqrt)
+        rows = const.tile([P, 3 * D], BF16, name="rows")
+        nc.vector.memset(rows[:], 0.0)
+        ones = const.tile([P, P], BF16, name="ones")
+        nc.vector.memset(ones[:], 1.0)
+        ident_f = const.tile([P, P], F32, name="ident_f")
+        make_identity(nc, ident_f[:])
+        ident_b = const.tile([P, P], BF16, name="ident_b")
+        make_identity(nc, ident_b[:])
+
+        w_sb = const.tile([P, 4 * D], BF16, name="w_sb")
+        nc.sync.dma_start(out=w_sb[:], in_=w_v.rearrange("(p t) k -> p (t k)", t=4))
+        load_chunk(kv_view, kv_tiles, "kv", 0)
+        aw_sb = const.tile([P, NT * 8], BF16, name="aw_sb")
+        nc.sync.dma_start(out=aw_sb[:], in_=attn_w.rearrange("(p j) h o -> p (j h o)", j=NT))
+        bv_bf = const.tile([P, 4], BF16, name="bv_bf")
+        nc.sync.dma_start(out=bv_bf[:], in_=b_v.rearrange("(p t) -> p t", t=4))
+        for i, vec in enumerate((ln_g, ln_b, out_b)):
+            nc.sync.dma_start(
+                out=rows[0:1, i * D : (i + 1) * D], in_=vec.rearrange("(o n) -> o n", o=1)
+            )
+        ow_sb = const.tile([P, 4 * D], BF16, name="ow_sb")
+        nc.sync.dma_start(
+            out=ow_sb[:].rearrange("p (nb d) -> p nb d", nb=4),
+            in_=out_w.rearrange("(nb p) d -> p nb d", p=P),
+        )
+        load_chunk(q_view, q_tiles, "q", 0)
+        load_chunk(kv_view, kv_tiles, "kv", 1)
+        load_chunk(q_view, q_tiles, "q", 1)
+        load_chunk(kv_view, kv_tiles, "kv", 2)
+        load_chunk(q_view, q_tiles, "q", 2)
+
+        bv = const.tile([P, 4], F32, name="bv")
+        nc.vector.tensor_copy(out=bv[:], in_=bv_bf[:])
+
+        def quantise_weight(words, tags, prefix):
+            grouped = const.tile([P, 4 * D], BF16, name=prefix + "g", align_bytes=64)
+            grouped_f = grouped[:].bitcast(F32)
+            for b in range(2):
+                bank = psum.tile([P, D], F32, name=prefix + "T%d" % b, tag=tags[b])
+                for s in range(2):
+                    for h in range(2):
+                        nc.tensor.transpose(
+                            bank[:, (s * 2 + h) * P : (s * 2 + h + 1) * P],
+                            words(2 * b + s, h),
+                            ident_f[:],
+                        )
+                nc.scalar.copy(
+                    out=grouped_f[:, b * D : (b + 1) * D].rearrange(
+                        "w (s c h) -> w s c h", s=2, h=2
+                    ),
+                    in_=bank[:].rearrange("w (s h c) -> w s c h", s=2, h=2),
+                )
+            codes = const.tile([P, D], U32, name=prefix + "c", align_bytes=64)
+            scales = const.tile([P, D], U8, name=prefix + "s", align_bytes=64)
+            nc.vector.quantize_mx(out=codes[:].bitcast(FP8X4), scales=scales[:], in_=grouped[:])
+            return codes, scales
+
+        w_f = w_sb[:].bitcast(F32)
+        wc, ws = quantise_weight(
+            lambda t, u: w_f[:, t * 256 + u * P : t * 256 + (u + 1) * P], ("s1a", "s1b"), "w"
+        )
+
+        g_ps = psum.tile([P, D], F32, name="g_ps", tag="g_ps")
+        nc.tensor.matmul(out=g_ps[:], lhsT=ones[:], rhs=rows[:, 0:D], start=True, stop=True)
+        b_ps = psum.tile([P, D], F32, name="b_ps", tag="b_ps")
+        nc.tensor.matmul(out=b_ps[:], lhsT=ones[:], rhs=rows[:, D : 2 * D], start=True, stop=True)
+        ob_ps = psum.tile([P, D], F32, name="ob_ps", tag="kvT")
+        nc.tensor.matmul(
+            out=ob_ps[:], lhsT=ones[:], rhs=rows[:, 2 * D : 3 * D], start=True, stop=True
+        )
+        ob_sb = const.tile([P, D], BF16, name="ob_sb")
+        nc.scalar.copy(out=ob_sb[:], in_=ob_ps[:])
+
+        ow_f = ow_sb[:].bitcast(F32).rearrange("n (nb q a) -> n nb a q", nb=4, a=2)
+        oc, os_ = quantise_weight(lambda nb, a: ow_f[:, nb, a, :], ("s2a", "s2b"), "o")
+
+        st = {}
+
+        def head_weights(blk):
+            awx = w2.tile([P, BLK * P], BF16, name="awx", tag="awx")
+            nc.gpsimd.tensor_scalar(
+                out=awx[:].rearrange("p (m r) -> p m r", r=16),
+                in0=aw_sb[:, blk * 64 : (blk + 1) * 64].unsqueeze(2).to_broadcast([P, 64, 16]),
+                scalar1=1.0,
+                scalar2=0.0,
+                op0=ALU.mult,
+                op1=ALU.add,
+            )
+            awT = psum.tile([P, BLK * P], BF16, name="awT", tag="awT")
+            for j in range(BLK):
+                nc.tensor.transpose(
+                    awT[:, j * P : (j + 1) * P], awx[:, j * P : (j + 1) * P], ident_b[:]
+                )
+            awE = w2.tile([P, BLK * P], BF16, name="awE", tag="awE")
+            nc.scalar.copy(out=awE[:], in_=awT[:])
+            st["awE", blk] = awE
+
+        def residual(c):
+            qp = w3.tile([P, GW], F32, name="qp", tag="qp")
+            t, off = q_tiles[GT * c]
+            nc.gpsimd.tensor_tensor(
+                out=qp[:].rearrange("p (j n) -> p j n", j=GT),
+                in0=t[:, off : off + GW].rearrange("p (j n) -> p j n", j=GT),
+                in1=ob_sb[:].unsqueeze(1).to_broadcast([P, GT, D]),
+                op=ALU.add,
+            )
+            st["qp", c] = qp
+
+        def transpose_kv(c):
+            kvT = psum.tile([P, D], F32, name="kvT", tag="kvT")
+            for jj in range(GT):
+                t, off = kv_tiles[GT * c + jj]
+                t_f = t[:].bitcast(F32)
+                for u in range(2):
+                    lo = off // 2 + u * P
+                    nc.tensor.transpose(
+                        kvT[:, (jj * 2 + u) * P : (jj * 2 + u + 1) * P],
+                        t_f[:, lo : lo + P],
+                        ident_f[:],
+                    )
+            kvg = w2.tile([P, 4 * GC], BF16, name="kvg", tag="kvg", align_bytes=64)
+            nc.scalar.copy(
+                out=kvg[:].bitcast(F32).rearrange("w (s c h) -> w s c h", s=GT, h=2),
+                in_=kvT[:].rearrange("w (s h c) -> w s c h", s=GT, h=2),
+            )
+            st["kvg", c] = kvg
+
+        def first_matmul(c):
+            kc = w2.tile([P, GC], U32, name="kc", tag="kc", align_bytes=64)
+            ks = w2.tile([P, GC], U8, name="ks", tag="ks", align_bytes=64)
+            nc.vector.quantize_mx(
+                out=kc[:].bitcast(FP8X4), scales=ks[:], in_=st["kvg", c][:]
+            )
+            banks = (
+                psum.tile([P, D], F32, name="s1a", tag="s1a"),
+                psum.tile([P, D], F32, name="s1b", tag="s1b"),
+            )
+            for t in range(4):
+                nc.tensor.matmul_mx(
+                    out=banks[t // 2][:, (t % 2) * GC : (t % 2 + 1) * GC],
+                    lhsT=wc[:, t * P : (t + 1) * P].bitcast(FP8X4),
+                    lhsT_scale=ws[:, t * P : (t + 1) * P],
+                    rhs=kc[:].bitcast(FP8X4),
+                    rhs_scale=ks[:],
+                    start=True,
+                    stop=True,
+                )
+            st["s1", c] = banks
+
+        def weigh_heads(c):
+            banks = st["s1", c]
+            awE = st["awE", (GT * c) // BLK]
+            lo = ((GT * c) % BLK) * P
+            planes = w2.tile([P, 4 * GC], BF16, name="planes", tag="planes")
+            for t in range(4):
+                nc.vector.scalar_tensor_tensor(
+                    out=planes[:, t * GC : (t + 1) * GC],
+                    in0=banks[t // 2][:, (t % 2) * GC : (t % 2 + 1) * GC],
+                    scalar=bv[:, t : t + 1],
+                    in1=awE[:, lo : lo + GC],
+                    op0=ALU.add,
+                    op1=ALU.mult,
+                )
+            ag = w2.tile([P, 4 * GC], BF16, name="ag", tag="ag", align_bytes=64)
+            nc.scalar.copy(
+                out=ag[:].rearrange("p (c i t) -> p c t i", i=4, t=4),
+                in_=planes[:].rearrange("p (t c i) -> p c t i", t=4, i=4),
+            )
+            st["ag", c] = ag
+
+        def second_matmul(c):
+            ac = w2.tile([P, GC], U32, name="ac", tag="ac", align_bytes=64)
+            asc = w2.tile([P, GC], U8, name="asc", tag="asc", align_bytes=64)
+            nc.vector.quantize_mx(
+                out=ac[:].bitcast(FP8X4), scales=asc[:], in_=st["ag", c][:]
+            )
+            banks = (
+                psum.tile([P, D], F32, name="s2a", tag="s2a"),
+                psum.tile([P, D], F32, name="s2b", tag="s2b"),
+            )
+            for jj in range(GT):
+                nc.tensor.matmul_mx(
+                    out=banks[jj][:],
+                    lhsT=ac[:, jj * P : (jj + 1) * P].bitcast(FP8X4),
+                    lhsT_scale=asc[:, jj * P : (jj + 1) * P],
+                    rhs=oc[:].bitcast(FP8X4),
+                    rhs_scale=os_[:],
+                    start=True,
+                    stop=True,
+                )
+            st["s2", c] = banks
+
+        def add_residual(c):
+            banks = st["s2", c]
+            qp = st["qp", c]
+            z = w2.tile([P, GW], F32, name="z", tag="z")
+            sums = w2.tile([P, GT], F32, name="sums", tag="sums")
+            for jj in range(GT):
+                nc.vector.scalar_tensor_tensor(
+                    out=z[:, jj * D : (jj + 1) * D],
+                    in0=banks[jj][:],
+                    scalar=0.0,
+                    in1=qp[:, jj * D : (jj + 1) * D],
+                    op0=ALU.add,
+                    op1=ALU.add,
+                    accum_out=sums[:, jj : jj + 1],
+                )
+            negmu = w2.tile([P, GT], F32, name="negmu", tag="negmu")
+            nc.scalar.mul(out=negmu[:], in_=sums[:], mul=-1.0 / D)
+            ssq = w2.tile([P, GT], F32, name="ssq", tag="ssq")
+            for jj in range(GT):
+                junk = w2.tile([P, D], BF16, name="junk", tag="junk")
+                nc.scalar.activation(
+                    out=junk[:],
+                    in_=z[:, jj * D : (jj + 1) * D],
+                    func=ACT.Square,
+                    bias=negmu[:, jj : jj + 1],
+                    scale=1.0,
+                    accum_out=ssq[:, jj : jj + 1],
+                )
+            std = w2.tile([P, GT], F32, name="std", tag="std")
+            nc.scalar.activation(
+                out=std[:], in_=ssq[:], func=ACT.Sqrt, bias=eps[:, 0:1], scale=1.0 / D
+            )
+            st["z", c] = (z, negmu, std)
+
+        def normalise(c):
+            z, negmu, std = st["z", c]
+            o = w3.tile([P, GW], F32, name="o", tag="o")
+            for jj in range(GT):
+                nc.vector.scalar_tensor_tensor(
+                    out=o[:, jj * D : (jj + 1) * D],
+                    in0=z[:, jj * D : (jj + 1) * D],
+                    scalar=negmu[:, jj : jj + 1],
+                    in1=g_ps[:],
+                    op0=ALU.add,
+                    op1=ALU.mult,
+                )
+            rstd = w2.tile([P, GT], F32, name="rstd", tag="rstd")
+            nc.vector.reciprocal(out=rstd[:], in_=std[:])
+            for jj in range(GT):
+                nc.vector.scalar_tensor_tensor(
+                    out=o[:, jj * D : (jj + 1) * D],
+                    in0=o[:, jj * D : (jj + 1) * D],
+                    scalar=rstd[:, jj : jj + 1],
+                    in1=b_ps[:],
+                    op0=ALU.mult,
+                    op1=ALU.add,
+                )
+            nc.sync.dma_start(out=out_view[:, c * GW : (c + 1) * GW], in_=o[:])
+
+        head_weights(0)
+        transpose_kv(0)
+        for tick in range(NG + 5):
+            if tick % 4 == 0 and tick // 4 + 3 < len(chunks):
+                load_chunk(kv_view, kv_tiles, "kv", tick // 4 + 3)
+                load_chunk(q_view, q_tiles, "q", tick // 4 + 3)
+            if tick + 1 < NG:
+                transpose_kv(tick + 1)
+            if (tick + 2) % 4 == 0 and (tick + 2) // 4 < NT // BLK:
+                head_weights((tick + 2) // 4)
+            if 0 <= tick - 1 < NG:
+                residual(tick - 1)
+            if 0 <= tick - 4 < NG:
+                normalise(tick - 4)
+            if 0 <= tick - 3 < NG:
+                add_residual(tick - 3)
+            if 0 <= tick - 1 < NG:
+                weigh_heads(tick - 1)
+            if tick < NG:
+                first_matmul(tick)
+            if 0 <= tick - 2 < NG:
+                second_matmul(tick - 2)

@@ -55,7 +55,7 @@ def tile_crossmodalattention_pa_t_kernel(
         eps = const.tile([P, 1], F32, name="eps")
         nc.vector.memset(eps[:], LN_EPS)
         warm = const.tile([P, 1], F32, name="warm")
-        nc.scalar.activation(out=warm[:], in_=eps[:], func=ACT.Sqrt)
+        nc.scalar.activation(out=warm[:], in_=eps[:], func=ACT.Abs_reciprocal_sqrt)
         rows = const.tile([P, 3 * D], BF16, name="rows")
         nc.vector.memset(rows[:], 0.0)
         ones = const.tile([P, P], BF16, name="ones")
@@ -156,6 +156,7 @@ def tile_crossmodalattention_pa_t_kernel(
         def residual(c):
             qp = w3.tile([P, GW], F32, name="qp", tag="qp")
             t, off = q_tiles[GT * c]
+            nc.vector.memset(qp[:, 0:1], 0.0)
             nc.gpsimd.tensor_tensor(
                 out=qp[:].rearrange("p (j n) -> p j n", j=GT),
                 in0=t[:, off : off + GW].rearrange("p (j n) -> p j n", j=GT),
@@ -276,14 +277,18 @@ def tile_crossmodalattention_pa_t_kernel(
                     scale=1.0,
                     accum_out=ssq[:, jj : jj + 1],
                 )
-            std = w2.tile([P, GT], F32, name="std", tag="std")
+            rstd = w2.tile([P, GT], F32, name="rstd", tag="rstd")
             nc.scalar.activation(
-                out=std[:], in_=ssq[:], func=ACT.Sqrt, bias=eps[:, 0:1], scale=1.0 / D
+                out=rstd[:],
+                in_=ssq[:],
+                func=ACT.Abs_reciprocal_sqrt,
+                bias=eps[:, 0:1],
+                scale=1.0 / D,
             )
-            st["z", c] = (z, negmu, std)
+            st["z", c] = (z, negmu, rstd)
 
-        def normalise(c):
-            z, negmu, std = st["z", c]
+        def centre(c):
+            z, negmu, rstd = st["z", c]
             o = w3.tile([P, GW], F32, name="o", tag="o")
             for jj in range(GT):
                 nc.vector.scalar_tensor_tensor(
@@ -294,8 +299,11 @@ def tile_crossmodalattention_pa_t_kernel(
                     op0=ALU.add,
                     op1=ALU.mult,
                 )
-            rstd = w2.tile([P, GT], F32, name="rstd", tag="rstd")
-            nc.vector.reciprocal(out=rstd[:], in_=std[:])
+            st["o", c] = o
+
+        def finish(c):
+            z, negmu, rstd = st["z", c]
+            o = st["o", c]
             for jj in range(GT):
                 nc.vector.scalar_tensor_tensor(
                     out=o[:, jj * D : (jj + 1) * D],
@@ -309,7 +317,8 @@ def tile_crossmodalattention_pa_t_kernel(
 
         head_weights(0)
         transpose_kv(0)
-        for tick in range(NG + 5):
+        residual(0)
+        for tick in range(NG + 4):
             if tick % 4 == 0 and tick // 4 + 3 < len(chunks):
                 load_chunk(kv_view, kv_tiles, "kv", tick // 4 + 3)
                 load_chunk(q_view, q_tiles, "q", tick // 4 + 3)
@@ -317,15 +326,17 @@ def tile_crossmodalattention_pa_t_kernel(
                 transpose_kv(tick + 1)
             if (tick + 2) % 4 == 0 and (tick + 2) // 4 < NT // BLK:
                 head_weights((tick + 2) // 4)
-            if 0 <= tick - 1 < NG:
-                residual(tick - 1)
-            if 0 <= tick - 4 < NG:
-                normalise(tick - 4)
             if 0 <= tick - 3 < NG:
-                add_residual(tick - 3)
+                centre(tick - 3)
             if 0 <= tick - 1 < NG:
                 weigh_heads(tick - 1)
+            if 0 <= tick - 3 < NG:
+                finish(tick - 3)
+            if 0 <= tick - 2 < NG:
+                add_residual(tick - 2)
             if tick < NG:
                 first_matmul(tick)
-            if 0 <= tick - 2 < NG:
-                second_matmul(tick - 2)
+            if 0 <= tick - 1 < NG:
+                second_matmul(tick - 1)
+            if tick + 1 < NG:
+                residual(tick + 1)

@@ -23,6 +23,7 @@ BLK = 8
 LN_EPS = 1e-5
 FLOPS = 2 * 2 * B * D * D
 PINNED = True
+G_TILES = 1
 
 
 def tile_crossmodalattention_pa_t_kernel(
@@ -35,6 +36,7 @@ def tile_crossmodalattention_pa_t_kernel(
         const = ctx.enter_context(tc.tile_pool(name="const", bufs=1))
         w2 = ctx.enter_context(tc.tile_pool(name="w2", bufs=2))
         w3 = ctx.enter_context(tc.tile_pool(name="w3", bufs=3))
+        w4 = ctx.enter_context(tc.tile_pool(name="w4", bufs=4))
         psum = ctx.enter_context(tc.psum_pool(name="psum", bufs=1))
 
         kv_view = kv_in.rearrange("(p j) k -> p (j k)", j=NT)
@@ -122,6 +124,10 @@ def tile_crossmodalattention_pa_t_kernel(
         nc.tensor.matmul(out=g_ps[:], lhsT=ones[:], rhs=rows[:, 0:D], start=True, stop=True)
         b_ps = psum.tile([P, D], F32, name="b_ps", tag="b_ps")
         nc.tensor.matmul(out=b_ps[:], lhsT=ones[:], rhs=rows[:, D : 2 * D], start=True, stop=True)
+        b2_ps = psum.tile([P, D], F32, name="b2_ps", tag="awT")
+        nc.tensor.matmul(out=b2_ps[:], lhsT=ones[:], rhs=rows[:, D : 2 * D], start=True, stop=True)
+        b_sb = const.tile([P, D], F32, name="b_sb")
+        nc.scalar.copy(out=b_sb[:], in_=b2_ps[:])
         ob_ps = psum.tile([P, D], F32, name="ob_ps", tag="kvT")
         nc.tensor.matmul(
             out=ob_ps[:], lhsT=ones[:], rhs=rows[:, 2 * D : 3 * D], start=True, stop=True
@@ -134,16 +140,16 @@ def tile_crossmodalattention_pa_t_kernel(
 
         st = {}
 
-        def head_weights(blk):
+        def expand_head_weights(blk):
             awx = w2.tile([P, BLK * P], BF16, name="awx", tag="awx")
-            nc.gpsimd.tensor_scalar(
+            nc.scalar.copy(
                 out=awx[:].rearrange("p (m r) -> p m r", r=16),
-                in0=aw_sb[:, blk * 64 : (blk + 1) * 64].unsqueeze(2).to_broadcast([P, 64, 16]),
-                scalar1=1.0,
-                scalar2=0.0,
-                op0=ALU.mult,
-                op1=ALU.add,
+                in_=aw_sb[:, blk * 64 : (blk + 1) * 64].unsqueeze(2).to_broadcast([P, 64, 16]),
             )
+            st["awx", blk] = awx
+
+        def head_weights(blk):
+            awx = st["awx", blk]
             awT = psum.tile([P, BLK * P], BF16, name="awT", tag="awT")
             for j in range(BLK):
                 nc.tensor.transpose(
@@ -289,7 +295,7 @@ def tile_crossmodalattention_pa_t_kernel(
 
         def centre(c):
             z, negmu, rstd = st["z", c]
-            o = w3.tile([P, GW], F32, name="o", tag="o")
+            o = w4.tile([P, GW], F32, name="o", tag="o")
             for jj in range(GT):
                 nc.vector.scalar_tensor_tensor(
                     out=o[:, jj * D : (jj + 1) * D],
@@ -299,12 +305,26 @@ def tile_crossmodalattention_pa_t_kernel(
                     op0=ALU.add,
                     op1=ALU.mult,
                 )
+            for jj in range(GT - G_TILES, GT):
+                nc.scalar.activation(
+                    out=o[:, jj * D : (jj + 1) * D],
+                    in_=o[:, jj * D : (jj + 1) * D],
+                    func=ACT.Copy,
+                    scale=rstd[:, jj : jj + 1],
+                )
             st["o", c] = o
 
         def finish(c):
             z, negmu, rstd = st["z", c]
             o = st["o", c]
-            for jj in range(GT):
+            for jj in range(GT - G_TILES, GT):
+                nc.gpsimd.tensor_tensor(
+                    out=o[:, jj * D : (jj + 1) * D],
+                    in0=o[:, jj * D : (jj + 1) * D],
+                    in1=b_sb[:],
+                    op=ALU.add,
+                )
+            for jj in range(GT - G_TILES):
                 nc.vector.scalar_tensor_tensor(
                     out=o[:, jj * D : (jj + 1) * D],
                     in0=o[:, jj * D : (jj + 1) * D],
@@ -315,10 +335,10 @@ def tile_crossmodalattention_pa_t_kernel(
                 )
             nc.sync.dma_start(out=out_view[:, c * GW : (c + 1) * GW], in_=o[:])
 
+        expand_head_weights(0)
         head_weights(0)
         transpose_kv(0)
-        residual(0)
-        for tick in range(NG + 4):
+        for tick in range(NG + 5):
             if tick % 4 == 0 and tick // 4 + 3 < len(chunks):
                 load_chunk(kv_view, kv_tiles, "kv", tick // 4 + 3)
                 load_chunk(q_view, q_tiles, "q", tick // 4 + 3)
@@ -326,17 +346,19 @@ def tile_crossmodalattention_pa_t_kernel(
                 transpose_kv(tick + 1)
             if (tick + 2) % 4 == 0 and (tick + 2) // 4 < NT // BLK:
                 head_weights((tick + 2) // 4)
-            if 0 <= tick - 3 < NG:
-                centre(tick - 3)
-            if 0 <= tick - 1 < NG:
-                weigh_heads(tick - 1)
-            if 0 <= tick - 3 < NG:
-                finish(tick - 3)
-            if 0 <= tick - 2 < NG:
-                add_residual(tick - 2)
+            if (tick + 3) % 4 == 0 and (tick + 3) // 4 < NT // BLK:
+                expand_head_weights((tick + 3) // 4)
             if tick < NG:
                 first_matmul(tick)
-            if 0 <= tick - 1 < NG:
-                second_matmul(tick - 1)
-            if tick + 1 < NG:
-                residual(tick + 1)
+            if 0 <= tick - 2 < NG:
+                second_matmul(tick - 2)
+            if tick < NG:
+                residual(tick)
+            if 0 <= tick - 4 < NG:
+                finish(tick - 4)
+            if 0 <= tick - 3 < NG:
+                centre(tick - 3)
+            if tick < NG:
+                weigh_heads(tick)
+            if 0 <= tick - 2 < NG:
+                add_residual(tick - 2)

@@ -23,7 +23,7 @@ BLK = 8
 LN_EPS = 1e-5
 FLOPS = 2 * 2 * B * D * D
 PINNED = True
-G_TILES = 1
+G_COLS = 384
 
 
 def tile_crossmodalattention_pa_t_kernel(
@@ -293,6 +293,10 @@ def tile_crossmodalattention_pa_t_kernel(
             )
             st["z", c] = (z, negmu, rstd)
 
+        def gpsimd_cols(c):
+            lo = GW if c == NG - 1 else GW - G_COLS
+            return lo, GW
+
         def centre(c):
             z, negmu, rstd = st["z", c]
             o = w4.tile([P, GW], F32, name="o", tag="o")
@@ -305,31 +309,28 @@ def tile_crossmodalattention_pa_t_kernel(
                     op0=ALU.add,
                     op1=ALU.mult,
                 )
-            for jj in range(GT - G_TILES, GT):
+            lo, hi = gpsimd_cols(c)
+            if lo < hi:
                 nc.scalar.activation(
-                    out=o[:, jj * D : (jj + 1) * D],
-                    in_=o[:, jj * D : (jj + 1) * D],
-                    func=ACT.Copy,
-                    scale=rstd[:, jj : jj + 1],
+                    out=o[:, lo:hi], in_=o[:, lo:hi], func=ACT.Copy, scale=rstd[:, GT - 1 : GT]
                 )
             st["o", c] = o
 
         def finish(c):
             z, negmu, rstd = st["z", c]
             o = st["o", c]
-            for jj in range(GT - G_TILES, GT):
+            lo, hi = gpsimd_cols(c)
+            if lo < hi:
                 nc.gpsimd.tensor_tensor(
-                    out=o[:, jj * D : (jj + 1) * D],
-                    in0=o[:, jj * D : (jj + 1) * D],
-                    in1=b_sb[:],
-                    op=ALU.add,
+                    out=o[:, lo:hi], in0=o[:, lo:hi], in1=b_sb[:, lo - D : hi - D], op=ALU.add
                 )
-            for jj in range(GT - G_TILES):
+            for jj in range(GT):
+                a, b = jj * D, min((jj + 1) * D, lo)
                 nc.vector.scalar_tensor_tensor(
-                    out=o[:, jj * D : (jj + 1) * D],
-                    in0=o[:, jj * D : (jj + 1) * D],
+                    out=o[:, a:b],
+                    in0=o[:, a:b],
                     scalar=rstd[:, jj : jj + 1],
-                    in1=b_ps[:],
+                    in1=b_ps[:, 0 : b - a],
                     op0=ALU.mult,
                     op1=ALU.add,
                 )

@@ -23,7 +23,7 @@ BLK = 8
 LN_EPS = 1e-5
 FLOPS = 2 * 2 * B * D * D
 PINNED = True
-G_COLS = 384
+G_COLS = 512
 
 
 def tile_crossmodalattention_pa_t_kernel(
@@ -67,11 +67,11 @@ def tile_crossmodalattention_pa_t_kernel(
         ident_b = const.tile([P, P], BF16, name="ident_b")
         make_identity(nc, ident_b[:])
 
-        w_sb = const.tile([P, 4 * D], BF16, name="w_sb")
-        nc.sync.dma_start(out=w_sb[:], in_=w_v.rearrange("(p t) k -> p (t k)", t=4))
         load_chunk(kv_view, kv_tiles, "kv", 0)
         aw_sb = const.tile([P, NT * 8], BF16, name="aw_sb")
         nc.sync.dma_start(out=aw_sb[:], in_=attn_w.rearrange("(p j) h o -> p (j h o)", j=NT))
+        w_sb = const.tile([P, 4 * D], BF16, name="w_sb")
+        nc.sync.dma_start(out=w_sb[:], in_=w_v.rearrange("(p t) k -> p (t k)", t=4))
         bv_bf = const.tile([P, 4], BF16, name="bv_bf")
         nc.sync.dma_start(out=bv_bf[:], in_=b_v.rearrange("(p t) -> p t", t=4))
         for i, vec in enumerate((ln_g, ln_b, out_b)):
@@ -89,10 +89,7 @@ def tile_crossmodalattention_pa_t_kernel(
         load_chunk(kv_view, kv_tiles, "kv", 2)
         load_chunk(q_view, q_tiles, "q", 2)
 
-        bv = const.tile([P, 4], F32, name="bv")
-        nc.vector.tensor_copy(out=bv[:], in_=bv_bf[:])
-
-        def quantise_weight(words, tags, prefix):
+        def weight_words(words, tags, prefix):
             grouped = const.tile([P, 4 * D], BF16, name=prefix + "g", align_bytes=64)
             grouped_f = grouped[:].bitcast(F32)
             for b in range(2):
@@ -110,33 +107,20 @@ def tile_crossmodalattention_pa_t_kernel(
                     ),
                     in_=bank[:].rearrange("w (s h c) -> w s c h", s=2, h=2),
                 )
+            return grouped
+
+        def quantise_weight(grouped, prefix):
             codes = const.tile([P, D], U32, name=prefix + "c", align_bytes=64)
             scales = const.tile([P, D], U8, name=prefix + "s", align_bytes=64)
             nc.vector.quantize_mx(out=codes[:].bitcast(FP8X4), scales=scales[:], in_=grouped[:])
             return codes, scales
 
-        w_f = w_sb[:].bitcast(F32)
-        wc, ws = quantise_weight(
-            lambda t, u: w_f[:, t * 256 + u * P : t * 256 + (u + 1) * P], ("s1a", "s1b"), "w"
-        )
-
-        g_ps = psum.tile([P, D], F32, name="g_ps", tag="g_ps")
-        nc.tensor.matmul(out=g_ps[:], lhsT=ones[:], rhs=rows[:, 0:D], start=True, stop=True)
-        b_ps = psum.tile([P, D], F32, name="b_ps", tag="b_ps")
-        nc.tensor.matmul(out=b_ps[:], lhsT=ones[:], rhs=rows[:, D : 2 * D], start=True, stop=True)
-        b2_ps = psum.tile([P, D], F32, name="b2_ps", tag="awT")
-        nc.tensor.matmul(out=b2_ps[:], lhsT=ones[:], rhs=rows[:, D : 2 * D], start=True, stop=True)
-        b_sb = const.tile([P, D], F32, name="b_sb")
-        nc.scalar.copy(out=b_sb[:], in_=b2_ps[:])
-        ob_ps = psum.tile([P, D], F32, name="ob_ps", tag="kvT")
-        nc.tensor.matmul(
-            out=ob_ps[:], lhsT=ones[:], rhs=rows[:, 2 * D : 3 * D], start=True, stop=True
-        )
-        ob_sb = const.tile([P, D], BF16, name="ob_sb")
-        nc.scalar.copy(out=ob_sb[:], in_=ob_ps[:])
-
-        ow_f = ow_sb[:].bitcast(F32).rearrange("n (nb q a) -> n nb a q", nb=4, a=2)
-        oc, os_ = quantise_weight(lambda nb, a: ow_f[:, nb, a, :], ("s2a", "s2b"), "o")
+        def spread(i, tag, name):
+            bank = psum.tile([P, D], F32, name=name, tag=tag)
+            nc.tensor.matmul(
+                out=bank[:], lhsT=ones[:], rhs=rows[:, i * D : (i + 1) * D], start=True, stop=True
+            )
+            return bank
 
         st = {}
 
@@ -171,6 +155,23 @@ def tile_crossmodalattention_pa_t_kernel(
             )
             st["qp", c] = qp
 
+        def to_quantise(tick):
+            if ("qin", tick) not in st:
+                st["qin", tick] = w3.tile([P, 8 * GC], BF16, name="qin", tag="qin", align_bytes=64)
+            return st["qin", tick]
+
+        def quantise(tick):
+            lo = 0 if tick < NG else GC
+            hi = 2 * GC if tick >= 2 else GC
+            codes = w2.tile([P, 2 * GC], U32, name="codes", tag="codes", align_bytes=64)
+            scales = w2.tile([P, 2 * GC], U8, name="scales", tag="scales", align_bytes=64)
+            nc.vector.quantize_mx(
+                out=codes[:, lo:hi].bitcast(FP8X4),
+                scales=scales[:, lo:hi],
+                in_=to_quantise(tick)[:, 4 * lo : 4 * hi],
+            )
+            st["codes", tick] = (codes, scales)
+
         def transpose_kv(c):
             kvT = psum.tile([P, D], F32, name="kvT", tag="kvT")
             for jj in range(GT):
@@ -183,19 +184,15 @@ def tile_crossmodalattention_pa_t_kernel(
                         t_f[:, lo : lo + P],
                         ident_f[:],
                     )
-            kvg = w2.tile([P, 4 * GC], BF16, name="kvg", tag="kvg", align_bytes=64)
             nc.scalar.copy(
-                out=kvg[:].bitcast(F32).rearrange("w (s c h) -> w s c h", s=GT, h=2),
+                out=to_quantise(c)[:, 0 : 4 * GC]
+                .bitcast(F32)
+                .rearrange("w (s c h) -> w s c h", s=GT, h=2),
                 in_=kvT[:].rearrange("w (s h c) -> w s c h", s=GT, h=2),
             )
-            st["kvg", c] = kvg
 
         def first_matmul(c):
-            kc = w2.tile([P, GC], U32, name="kc", tag="kc", align_bytes=64)
-            ks = w2.tile([P, GC], U8, name="ks", tag="ks", align_bytes=64)
-            nc.vector.quantize_mx(
-                out=kc[:].bitcast(FP8X4), scales=ks[:], in_=st["kvg", c][:]
-            )
+            codes, scales = st["codes", c]
             banks = (
                 psum.tile([P, D], F32, name="s1a", tag="s1a"),
                 psum.tile([P, D], F32, name="s1b", tag="s1b"),
@@ -205,8 +202,8 @@ def tile_crossmodalattention_pa_t_kernel(
                     out=banks[t // 2][:, (t % 2) * GC : (t % 2 + 1) * GC],
                     lhsT=wc[:, t * P : (t + 1) * P].bitcast(FP8X4),
                     lhsT_scale=ws[:, t * P : (t + 1) * P],
-                    rhs=kc[:].bitcast(FP8X4),
-                    rhs_scale=ks[:],
+                    rhs=codes[:, 0:GC].bitcast(FP8X4),
+                    rhs_scale=scales[:, 0:GC],
                     start=True,
                     stop=True,
                 )
@@ -226,19 +223,15 @@ def tile_crossmodalattention_pa_t_kernel(
                     op0=ALU.add,
                     op1=ALU.mult,
                 )
-            ag = w2.tile([P, 4 * GC], BF16, name="ag", tag="ag", align_bytes=64)
             nc.scalar.copy(
-                out=ag[:].rearrange("p (c i t) -> p c t i", i=4, t=4),
+                out=to_quantise(c + 2)[:, 4 * GC : 8 * GC].rearrange(
+                    "p (c i t) -> p c t i", i=4, t=4
+                ),
                 in_=planes[:].rearrange("p (t c i) -> p c t i", t=4, i=4),
             )
-            st["ag", c] = ag
 
         def second_matmul(c):
-            ac = w2.tile([P, GC], U32, name="ac", tag="ac", align_bytes=64)
-            asc = w2.tile([P, GC], U8, name="asc", tag="asc", align_bytes=64)
-            nc.vector.quantize_mx(
-                out=ac[:].bitcast(FP8X4), scales=asc[:], in_=st["ag", c][:]
-            )
+            codes, scales = st["codes", c + 2]
             banks = (
                 psum.tile([P, D], F32, name="s2a", tag="s2a"),
                 psum.tile([P, D], F32, name="s2b", tag="s2b"),
@@ -246,8 +239,8 @@ def tile_crossmodalattention_pa_t_kernel(
             for jj in range(GT):
                 nc.tensor.matmul_mx(
                     out=banks[jj][:],
-                    lhsT=ac[:, jj * P : (jj + 1) * P].bitcast(FP8X4),
-                    lhsT_scale=asc[:, jj * P : (jj + 1) * P],
+                    lhsT=codes[:, GC + jj * P : GC + (jj + 1) * P].bitcast(FP8X4),
+                    lhsT_scale=scales[:, GC + jj * P : GC + (jj + 1) * P],
                     rhs=oc[:].bitcast(FP8X4),
                     rhs_scale=os_[:],
                     start=True,
@@ -326,19 +319,35 @@ def tile_crossmodalattention_pa_t_kernel(
                 )
             for jj in range(GT):
                 a, b = jj * D, min((jj + 1) * D, lo)
-                nc.vector.scalar_tensor_tensor(
-                    out=o[:, a:b],
-                    in0=o[:, a:b],
-                    scalar=rstd[:, jj : jj + 1],
-                    in1=b_ps[:, 0 : b - a],
-                    op0=ALU.mult,
-                    op1=ALU.add,
-                )
+                if a < b:
+                    nc.vector.scalar_tensor_tensor(
+                        out=o[:, a:b],
+                        in0=o[:, a:b],
+                        scalar=rstd[:, jj : jj + 1],
+                        in1=b_ps[:, 0 : b - a],
+                        op0=ALU.mult,
+                        op1=ALU.add,
+                    )
             nc.sync.dma_start(out=out_view[:, c * GW : (c + 1) * GW], in_=o[:])
 
         expand_head_weights(0)
-        head_weights(0)
         transpose_kv(0)
+        w_f = w_sb[:].bitcast(F32)
+        wg = weight_words(
+            lambda t, u: w_f[:, t * 256 + u * P : t * 256 + (u + 1) * P], ("s1a", "s1b"), "w"
+        )
+        wc, ws = quantise_weight(wg, "w")
+        head_weights(0)
+        bv = const.tile([P, 4], F32, name="bv")
+        nc.vector.tensor_copy(out=bv[:], in_=bv_bf[:])
+        ob_ps = spread(2, "kvT", "ob_ps")
+        ob_sb = const.tile([P, D], BF16, name="ob_sb")
+        nc.scalar.copy(out=ob_sb[:], in_=ob_ps[:])
+        g_ps = spread(0, "g_ps", "g_ps")
+        b_ps = spread(1, "b_ps", "b_ps")
+        ow_f = ow_sb[:].bitcast(F32).rearrange("n (nb q a) -> n nb a q", nb=4, a=2)
+        b_sb = const.tile([P, D], F32, name="b_sb")
+
         for tick in range(NG + 5):
             if tick % 4 == 0 and tick // 4 + 3 < len(chunks):
                 load_chunk(kv_view, kv_tiles, "kv", tick // 4 + 3)
@@ -349,8 +358,12 @@ def tile_crossmodalattention_pa_t_kernel(
                 head_weights((tick + 2) // 4)
             if (tick + 3) % 4 == 0 and (tick + 3) // 4 < NT // BLK:
                 expand_head_weights((tick + 3) // 4)
+            if tick < NG + 2:
+                quantise(tick)
             if tick < NG:
                 first_matmul(tick)
+            if tick == 1:
+                oc, os_ = quantise_weight(og, "o")
             if 0 <= tick - 2 < NG:
                 second_matmul(tick - 2)
             if tick < NG:
@@ -363,3 +376,7 @@ def tile_crossmodalattention_pa_t_kernel(
                 weigh_heads(tick)
             if 0 <= tick - 2 < NG:
                 add_residual(tick - 2)
+            if tick == 0:
+                og = weight_words(lambda nb, a: ow_f[:, nb, a, :], ("s2a", "s2b"), "o")
+                b2_ps = spread(1, "awT", "b2_ps")
+                nc.scalar.copy(out=b_sb[:], in_=b2_ps[:])

@@ -23,7 +23,7 @@ BLK = 8
 LN_EPS = 1e-5
 FLOPS = 2 * 2 * B * D * D
 PINNED = True
-G_COLS = 512
+G_COLS = 640
 
 
 def tile_crossmodalattention_pa_t_kernel(
@@ -303,10 +303,12 @@ def tile_crossmodalattention_pa_t_kernel(
                     op1=ALU.mult,
                 )
             lo, hi = gpsimd_cols(c)
-            if lo < hi:
-                nc.scalar.activation(
-                    out=o[:, lo:hi], in_=o[:, lo:hi], func=ACT.Copy, scale=rstd[:, GT - 1 : GT]
-                )
+            for jj in range(GT):
+                a, b = max(jj * D, lo), (jj + 1) * D
+                if a < b:
+                    nc.scalar.activation(
+                        out=o[:, a:b], in_=o[:, a:b], func=ACT.Copy, scale=rstd[:, jj : jj + 1]
+                    )
             st["o", c] = o
 
         def finish(c):
@@ -315,7 +317,7 @@ def tile_crossmodalattention_pa_t_kernel(
             lo, hi = gpsimd_cols(c)
             if lo < hi:
                 nc.gpsimd.tensor_tensor(
-                    out=o[:, lo:hi], in0=o[:, lo:hi], in1=b_sb[:, lo - D : hi - D], op=ALU.add
+                    out=o[:, lo:hi], in0=o[:, lo:hi], in1=b_sb[:, lo:hi], op=ALU.add
                 )
             for jj in range(GT):
                 a, b = jj * D, min((jj + 1) * D, lo)
@@ -346,7 +348,7 @@ def tile_crossmodalattention_pa_t_kernel(
         g_ps = spread(0, "g_ps", "g_ps")
         b_ps = spread(1, "b_ps", "b_ps")
         ow_f = ow_sb[:].bitcast(F32).rearrange("n (nb q a) -> n nb a q", nb=4, a=2)
-        b_sb = const.tile([P, D], F32, name="b_sb")
+        b_sb = const.tile([P, GW], F32, name="b_sb")
 
         for tick in range(NG + 5):
             if tick % 4 == 0 and tick // 4 + 3 < len(chunks):
@@ -379,4 +381,5 @@ def tile_crossmodalattention_pa_t_kernel(
             if tick == 0:
                 og = weight_words(lambda nb, a: ow_f[:, nb, a, :], ("s2a", "s2b"), "o")
                 b2_ps = spread(1, "awT", "b2_ps")
-                nc.scalar.copy(out=b_sb[:], in_=b2_ps[:])
+                for jj in range(GT):
+                    nc.scalar.copy(out=b_sb[:, jj * D : (jj + 1) * D], in_=b2_ps[:])

@@ -360,6 +360,8 @@ def tile_crossmodalattention_pa_t_kernel(
                 head_weights((tick + 2) // 4)
             if (tick + 3) % 4 == 0 and (tick + 3) // 4 < NT // BLK:
                 expand_head_weights((tick + 3) // 4)
+            if tick < NG:
+                residual(tick)
             if tick < NG + 2:
                 quantise(tick)
             if tick < NG:
@@ -368,8 +370,6 @@ def tile_crossmodalattention_pa_t_kernel(
                 oc, os_ = quantise_weight(og, "o")
             if 0 <= tick - 2 < NG:
                 second_matmul(tick - 2)
-            if tick < NG:
-                residual(tick)
             if 0 <= tick - 4 < NG:
                 finish(tick - 4)
             if 0 <= tick - 3 < NG:

@@ -22,7 +22,7 @@ GC = GT * P
 BLK = 8
 LN_EPS = 1e-5
 FLOPS = 2 * 2 * B * D * D
-PINNED = True
+PINNED = False
 G_COLS = 640
 
 

from contextlib import ExitStack

import concourse.mybir as mybir
from concourse.masks import make_identity

F32 = mybir.dt.float32
BF16 = mybir.dt.bfloat16
U32 = mybir.dt.uint32
U8 = mybir.dt.uint8
FP8X4 = mybir.dt.float8_e4m3fn_x4
ALU = mybir.AluOpType
ACT = mybir.ActivationFunctionType

P = 128
B = 8192
D = 512
NT = B // P
GT = 2
NG = NT // GT
GW = GT * D
GC = GT * P
BLK = 8
LN_EPS = 1e-5
FLOPS = 2 * 2 * B * D * D
PINNED = False
G_COLS = 640


def tile_crossmodalattention_pa_t_kernel(
    tc, kv_in, q_in, attn_w, w_v, b_v, out_w, out_b, ln_g, ln_b, out
):
    nc = tc.nc
    with ExitStack() as ctx:
        if PINNED:
            ctx.enter_context(tc.manual_schedule())
        const = ctx.enter_context(tc.tile_pool(name="const", bufs=1))
        w2 = ctx.enter_context(tc.tile_pool(name="w2", bufs=2))
        w3 = ctx.enter_context(tc.tile_pool(name="w3", bufs=3))
        w4 = ctx.enter_context(tc.tile_pool(name="w4", bufs=4))
        psum = ctx.enter_context(tc.psum_pool(name="psum", bufs=1))

        kv_view = kv_in.rearrange("(p j) k -> p (j k)", j=NT)
        q_view = q_in.rearrange("(p j) k -> p (j k)", j=NT)
        out_view = out.rearrange("(p j) n -> p (j n)", j=NT)

        chunks = [(0, 2), (2, 8)] + [(a, a + 8) for a in range(8, NT, 8)]
        kv_tiles = {}
        q_tiles = {}

        def load_chunk(view, store, prefix, k):
            j0, j1 = chunks[k]
            t = const.tile([P, (j1 - j0) * D], BF16, name="%s%d" % (prefix, k))
            nc.sync.dma_start(out=t[:], in_=view[:, j0 * D : j1 * D])
            for j in range(j0, j1):
                store[j] = (t, (j - j0) * D)

        eps = const.tile([P, 1], F32, name="eps")
        nc.vector.memset(eps[:], LN_EPS)
        warm = const.tile([P, 1], F32, name="warm")
        nc.scalar.activation(out=warm[:], in_=eps[:], func=ACT.Abs_reciprocal_sqrt)
        rows = const.tile([P, 3 * D], BF16, name="rows")
        nc.vector.memset(rows[:], 0.0)
        ones = const.tile([P, P], BF16, name="ones")
        nc.vector.memset(ones[:], 1.0)
        ident_f = const.tile([P, P], F32, name="ident_f")
        make_identity(nc, ident_f[:])
        ident_b = const.tile([P, P], BF16, name="ident_b")
        make_identity(nc, ident_b[:])

        load_chunk(kv_view, kv_tiles, "kv", 0)
        aw_sb = const.tile([P, NT * 8], BF16, name="aw_sb")
        nc.sync.dma_start(out=aw_sb[:], in_=attn_w.rearrange("(p j) h o -> p (j h o)", j=NT))
        w_sb = const.tile([P, 4 * D], BF16, name="w_sb")
        nc.sync.dma_start(out=w_sb[:], in_=w_v.rearrange("(p t) k -> p (t k)", t=4))
        bv_bf = const.tile([P, 4], BF16, name="bv_bf")
        nc.sync.dma_start(out=bv_bf[:], in_=b_v.rearrange("(p t) -> p t", t=4))
        for i, vec in enumerate((ln_g, ln_b, out_b)):
            nc.sync.dma_start(
                out=rows[0:1, i * D : (i + 1) * D], in_=vec.rearrange("(o n) -> o n", o=1)
            )
        ow_sb = const.tile([P, 4 * D], BF16, name="ow_sb")
        nc.sync.dma_start(
            out=ow_sb[:].rearrange("p (nb d) -> p nb d", nb=4),
            in_=out_w.rearrange("(nb p) d -> p nb d", p=P),
        )
        load_chunk(q_view, q_tiles, "q", 0)
        load_chunk(kv_view, kv_tiles, "kv", 1)
        load_chunk(q_view, q_tiles, "q", 1)
        load_chunk(kv_view, kv_tiles, "kv", 2)
        load_chunk(q_view, q_tiles, "q", 2)

        def weight_words(words, tags, prefix):
            grouped = const.tile([P, 4 * D], BF16, name=prefix + "g", align_bytes=64)
            grouped_f = grouped[:].bitcast(F32)
            for b in range(2):
                bank = psum.tile([P, D], F32, name=prefix + "T%d" % b, tag=tags[b])
                for s in range(2):
                    for h in range(2):
                        nc.tensor.transpose(
                            bank[:, (s * 2 + h) * P : (s * 2 + h + 1) * P],
                            words(2 * b + s, h),
                            ident_f[:],
                        )
                nc.scalar.copy(
                    out=grouped_f[:, b * D : (b + 1) * D].rearrange(
                        "w (s c h) -> w s c h", s=2, h=2
                    ),
                    in_=bank[:].rearrange("w (s h c) -> w s c h", s=2, h=2),
                )
            return grouped

        def quantise_weight(grouped, prefix):
            codes = const.tile([P, D], U32, name=prefix + "c", align_bytes=64)
            scales = const.tile([P, D], U8, name=prefix + "s", align_bytes=64)
            nc.vector.quantize_mx(out=codes[:].bitcast(FP8X4), scales=scales[:], in_=grouped[:])
            return codes, scales

        def spread(i, tag, name):
            bank = psum.tile([P, D], F32, name=name, tag=tag)
            nc.tensor.matmul(
                out=bank[:], lhsT=ones[:], rhs=rows[:, i * D : (i + 1) * D], start=True, stop=True
            )
            return bank

        st = {}

        def expand_head_weights(blk):
            awx = w2.tile([P, BLK * P], BF16, name="awx", tag="awx")
            nc.scalar.copy(
                out=awx[:].rearrange("p (m r) -> p m r", r=16),
                in_=aw_sb[:, blk * 64 : (blk + 1) * 64].unsqueeze(2).to_broadcast([P, 64, 16]),
            )
            st["awx", blk] = awx

        def head_weights(blk):
            awx = st["awx", blk]
            awT = psum.tile([P, BLK * P], BF16, name="awT", tag="awT")
            for j in range(BLK):
                nc.tensor.transpose(
                    awT[:, j * P : (j + 1) * P], awx[:, j * P : (j + 1) * P], ident_b[:]
                )
            awE = w2.tile([P, BLK * P], BF16, name="awE", tag="awE")
            nc.scalar.copy(out=awE[:], in_=awT[:])
            st["awE", blk] = awE

        def residual(c):
            qp = w3.tile([P, GW], F32, name="qp", tag="qp")
            t, off = q_tiles[GT * c]
            nc.vector.memset(qp[:, 0:1], 0.0)
            nc.gpsimd.tensor_tensor(
                out=qp[:].rearrange("p (j n) -> p j n", j=GT),
                in0=t[:, off : off + GW].rearrange("p (j n) -> p j n", j=GT),
                in1=ob_sb[:].unsqueeze(1).to_broadcast([P, GT, D]),
                op=ALU.add,
            )
            st["qp", c] = qp

        def to_quantise(tick):
            if ("qin", tick) not in st:
                st["qin", tick] = w3.tile([P, 8 * GC], BF16, name="qin", tag="qin", align_bytes=64)
            return st["qin", tick]

        def quantise(tick):
            lo = 0 if tick < NG else GC
            hi = 2 * GC if tick >= 2 else GC
            codes = w2.tile([P, 2 * GC], U32, name="codes", tag="codes", align_bytes=64)
            scales = w2.tile([P, 2 * GC], U8, name="scales", tag="scales", align_bytes=64)
            nc.vector.quantize_mx(
                out=codes[:, lo:hi].bitcast(FP8X4),
                scales=scales[:, lo:hi],
                in_=to_quantise(tick)[:, 4 * lo : 4 * hi],
            )
            st["codes", tick] = (codes, scales)

        def transpose_kv(c):
            kvT = psum.tile([P, D], F32, name="kvT", tag="kvT")
            for jj in range(GT):
                t, off = kv_tiles[GT * c + jj]
                t_f = t[:].bitcast(F32)
                for u in range(2):
                    lo = off // 2 + u * P
                    nc.tensor.transpose(
                        kvT[:, (jj * 2 + u) * P : (jj * 2 + u + 1) * P],
                        t_f[:, lo : lo + P],
                        ident_f[:],
                    )
            nc.scalar.copy(
                out=to_quantise(c)[:, 0 : 4 * GC]
                .bitcast(F32)
                .rearrange("w (s c h) -> w s c h", s=GT, h=2),
                in_=kvT[:].rearrange("w (s h c) -> w s c h", s=GT, h=2),
            )

        def first_matmul(c):
            codes, scales = st["codes", c]
            banks = (
                psum.tile([P, D], F32, name="s1a", tag="s1a"),
                psum.tile([P, D], F32, name="s1b", tag="s1b"),
            )
            for t in range(4):
                nc.tensor.matmul_mx(
                    out=banks[t // 2][:, (t % 2) * GC : (t % 2 + 1) * GC],
                    lhsT=wc[:, t * P : (t + 1) * P].bitcast(FP8X4),
                    lhsT_scale=ws[:, t * P : (t + 1) * P],
                    rhs=codes[:, 0:GC].bitcast(FP8X4),
                    rhs_scale=scales[:, 0:GC],
                    start=True,
                    stop=True,
                )
            st["s1", c] = banks

        def weigh_heads(c):
            banks = st["s1", c]
            awE = st["awE", (GT * c) // BLK]
            lo = ((GT * c) % BLK) * P
            planes = w2.tile([P, 4 * GC], BF16, name="planes", tag="planes")
            for t in range(4):
                nc.vector.scalar_tensor_tensor(
                    out=planes[:, t * GC : (t + 1) * GC],
                    in0=banks[t // 2][:, (t % 2) * GC : (t % 2 + 1) * GC],
                    scalar=bv[:, t : t + 1],
                    in1=awE[:, lo : lo + GC],
                    op0=ALU.add,
                    op1=ALU.mult,
                )
            nc.scalar.copy(
                out=to_quantise(c + 2)[:, 4 * GC : 8 * GC].rearrange(
                    "p (c i t) -> p c t i", i=4, t=4
                ),
                in_=planes[:].rearrange("p (t c i) -> p c t i", t=4, i=4),
            )

        def second_matmul(c):
            codes, scales = st["codes", c + 2]
            banks = (
                psum.tile([P, D], F32, name="s2a", tag="s2a"),
                psum.tile([P, D], F32, name="s2b", tag="s2b"),
            )
            for jj in range(GT):
                nc.tensor.matmul_mx(
                    out=banks[jj][:],
                    lhsT=codes[:, GC + jj * P : GC + (jj + 1) * P].bitcast(FP8X4),
                    lhsT_scale=scales[:, GC + jj * P : GC + (jj + 1) * P],
                    rhs=oc[:].bitcast(FP8X4),
                    rhs_scale=os_[:],
                    start=True,
                    stop=True,
                )
            st["s2", c] = banks

        def add_residual(c):
            banks = st["s2", c]
            qp = st["qp", c]
            z = w2.tile([P, GW], F32, name="z", tag="z")
            sums = w2.tile([P, GT], F32, name="sums", tag="sums")
            for jj in range(GT):
                nc.vector.scalar_tensor_tensor(
                    out=z[:, jj * D : (jj + 1) * D],
                    in0=banks[jj][:],
                    scalar=0.0,
                    in1=qp[:, jj * D : (jj + 1) * D],
                    op0=ALU.add,
                    op1=ALU.add,
                    accum_out=sums[:, jj : jj + 1],
                )
            negmu = w2.tile([P, GT], F32, name="negmu", tag="negmu")
            nc.scalar.mul(out=negmu[:], in_=sums[:], mul=-1.0 / D)
            ssq = w2.tile([P, GT], F32, name="ssq", tag="ssq")
            for jj in range(GT):
                junk = w2.tile([P, D], BF16, name="junk", tag="junk")
                nc.scalar.activation(
                    out=junk[:],
                    in_=z[:, jj * D : (jj + 1) * D],
                    func=ACT.Square,
                    bias=negmu[:, jj : jj + 1],
                    scale=1.0,
                    accum_out=ssq[:, jj : jj + 1],
                )
            rstd = w2.tile([P, GT], F32, name="rstd", tag="rstd")
            nc.scalar.activation(
                out=rstd[:],
                in_=ssq[:],
                func=ACT.Abs_reciprocal_sqrt,
                bias=eps[:, 0:1],
                scale=1.0 / D,
            )
            st["z", c] = (z, negmu, rstd)

        def gpsimd_cols(c):
            lo = GW if c == NG - 1 else GW - G_COLS
            return lo, GW

        def centre(c):
            z, negmu, rstd = st["z", c]
            o = w4.tile([P, GW], F32, name="o", tag="o")
            for jj in range(GT):
                nc.vector.scalar_tensor_tensor(
                    out=o[:, jj * D : (jj + 1) * D],
                    in0=z[:, jj * D : (jj + 1) * D],
                    scalar=negmu[:, jj : jj + 1],
                    in1=g_ps[:],
                    op0=ALU.add,
                    op1=ALU.mult,
                )
            lo, hi = gpsimd_cols(c)
            for jj in range(GT):
                a, b = max(jj * D, lo), (jj + 1) * D
                if a < b:
                    nc.scalar.activation(
                        out=o[:, a:b], in_=o[:, a:b], func=ACT.Copy, scale=rstd[:, jj : jj + 1]
                    )
            st["o", c] = o

        def finish(c):
            z, negmu, rstd = st["z", c]
            o = st["o", c]
            lo, hi = gpsimd_cols(c)
            if lo < hi:
                nc.gpsimd.tensor_tensor(
                    out=o[:, lo:hi], in0=o[:, lo:hi], in1=b_sb[:, lo:hi], op=ALU.add
                )
            for jj in range(GT):
                a, b = jj * D, min((jj + 1) * D, lo)
                if a < b:
                    nc.vector.scalar_tensor_tensor(
                        out=o[:, a:b],
                        in0=o[:, a:b],
                        scalar=rstd[:, jj : jj + 1],
                        in1=b_ps[:, 0 : b - a],
                        op0=ALU.mult,
                        op1=ALU.add,
                    )
            nc.sync.dma_start(out=out_view[:, c * GW : (c + 1) * GW], in_=o[:])

        expand_head_weights(0)
        transpose_kv(0)
        w_f = w_sb[:].bitcast(F32)
        wg = weight_words(
            lambda t, u: w_f[:, t * 256 + u * P : t * 256 + (u + 1) * P], ("s1a", "s1b"), "w"
        )
        wc, ws = quantise_weight(wg, "w")
        head_weights(0)
        bv = const.tile([P, 4], F32, name="bv")
        nc.vector.tensor_copy(out=bv[:], in_=bv_bf[:])
        ob_ps = spread(2, "kvT", "ob_ps")
        ob_sb = const.tile([P, D], BF16, name="ob_sb")
        nc.scalar.copy(out=ob_sb[:], in_=ob_ps[:])
        g_ps = spread(0, "g_ps", "g_ps")
        b_ps = spread(1, "b_ps", "b_ps")
        ow_f = ow_sb[:].bitcast(F32).rearrange("n (nb q a) -> n nb a q", nb=4, a=2)
        b_sb = const.tile([P, GW], F32, name="b_sb")

        for tick in range(NG + 5):
            if tick % 4 == 0 and tick // 4 + 3 < len(chunks):
                load_chunk(kv_view, kv_tiles, "kv", tick // 4 + 3)
                load_chunk(q_view, q_tiles, "q", tick // 4 + 3)
            if tick + 1 < NG:
                transpose_kv(tick + 1)
            if (tick + 2) % 4 == 0 and (tick + 2) // 4 < NT // BLK:
                head_weights((tick + 2) // 4)
            if (tick + 3) % 4 == 0 and (tick + 3) // 4 < NT // BLK:
                expand_head_weights((tick + 3) // 4)
            if tick < NG:
                residual(tick)
            if tick < NG + 2:
                quantise(tick)
            if tick < NG:
                first_matmul(tick)
            if tick == 1:
                oc, os_ = quantise_weight(og, "o")
            if 0 <= tick - 2 < NG:
                second_matmul(tick - 2)
            if 0 <= tick - 4 < NG:
                finish(tick - 4)
            if 0 <= tick - 3 < NG:
                centre(tick - 3)
            if tick < NG:
                weigh_heads(tick)
            if 0 <= tick - 2 < NG:
                add_residual(tick - 2)
            if tick == 0:
                og = weight_words(lambda nb, a: ow_f[:, nb, a, :], ("s2a", "s2b"), "o")
                b2_ps = spread(1, "awT", "b2_ps")
                for jj in range(GT):
                    nc.scalar.copy(out=b_sb[:, jj * D : (jj + 1) * D], in_=b2_ps[:])
